import numpy as np
import ml_dtypes


def mxq(x, axis, fmt="e4m3"):
    dtype, down = {"e4m3": (ml_dtypes.float8_e4m3fn, 7), "e5m2": (ml_dtypes.float8_e5m2, 14)}[fmt]
    v = np.moveaxis(np.asarray(x, np.float32).astype(ml_dtypes.bfloat16).astype(np.float64), axis, -1)
    blocks = v.reshape(v.shape[:-1] + (-1, 32))
    amax = np.abs(blocks).max(-1, keepdims=True)
    byte = np.maximum(np.where(amax > 0, np.frexp(amax)[1] - 1 + 127, 0) - down, 1)
    scale = np.exp2(byte - 127.0)
    codes = (blocks / scale).astype(np.float32).astype(dtype).astype(np.float64)
    return np.moveaxis((codes * scale).reshape(v.shape), -1, axis)


WIDE = False


def mx_kscale(k):
    if not WIDE:
        return np.ones(k)
    levels = np.array([10, -10, 5, -5, 0])
    if k % 512:
        return np.exp2(np.random.permutation(np.resize(levels, k // 32))).repeat(32)
    a = np.empty((k // 512, 16))
    for p in range(k // 512):
        a[p, :8] = np.random.permutation(np.resize(levels, 8))
        for g in range(8):
            far = levels[np.abs(levels - a[p, g]) >= 10]
            a[p, g + 8] = far[np.random.randint(len(far))]
    return np.exp2(a.ravel()).repeat(32)


BF16 = ml_dtypes.bfloat16


def bf(x):
    return np.asarray(x, np.float32).astype(BF16)


def f64(x):
    return np.asarray(x).astype(np.float64)


B, C, T, H, W, AT, AF = 1, 1024, 8, 16, 16, 32, 64
D = C // 2
C2 = 2 * C
NKV = AT * AF
REP, REM = AT // T, AT % T
QS = np.sqrt(2.0 / np.sqrt(D))


def setup_inputs():
    s = mx_kscale(C2)
    sa, sv = s[:C], s[C:]
    m = np.random.standard_normal((B, C, T))[..., None, None]
    return {"v": bf((np.random.standard_normal((B, C, T, H, W)) + 0.7 * m) * sv[None, :, None, None, None]),
            "a": bf(np.random.standard_normal((B, C, AT, AF)) * sa[None, :, None, None]),
            "Wp": bf(np.random.standard_normal((D, C2)) * 0.8 * QS / np.sqrt(C) / s[None, :]),
            "bp": bf(np.random.standard_normal(D) * 0.1),
            "Wg": bf(np.random.standard_normal((D, C2)) / np.sqrt(C) / s[None, :]),
            "bg": bf(np.random.standard_normal(D) * 0.1)}


def reference(v, a, Wp, bp, Wg, bg):
    z = f64(v).mean(axis=(3, 4))
    z = np.repeat(z, REP, axis=2)
    if REM:
        z = np.concatenate([z, np.broadcast_to(z[:, :, -1:], (B, C, REM))], axis=2)
    z = np.broadcast_to(z[..., None], (B, C, AT, AF))
    av = np.concatenate([f64(a), z], axis=1).reshape(B, C2, NKV)
    avq = mxq(av, 1, "e4m3")
    phi_av = (mxq(f64(Wp), 1, "e4m3") @ avq) + f64(bp)[:, None]
    g_av = (mxq(f64(Wg), 1, "e4m3") @ avq) + f64(bg)[:, None]
    return phi_av, g_av.transpose(0, 2, 1)

@@ -1,0 +1,325 @@
+from contextlib import ExitStack
+
+import concourse.mybir as mybir
+from concourse.masks import make_identity
+
+F32 = mybir.dt.float32
+BF16 = mybir.dt.bfloat16
+I32 = mybir.dt.int32
+U32 = mybir.dt.uint32
+U8 = mybir.dt.uint8
+FP8X4 = mybir.dt.float8_e4m3fn_x4
+ADD = mybir.AluOpType.add
+MULT = mybir.AluOpType.mult
+IDENTITY = mybir.ActivationFunctionType.Identity
+
+P = 128
+C = 1024
+T = 8
+HW = 256
+N = 2048
+COLS_PER_T = N // T
+D = 512
+K_PASS = 512
+A_PASSES = C // K_PASS
+Z_PASSES = C // K_PASS
+SLABS = C // (2 * P)
+N_TILE = 512
+CHUNKS = N // N_TILE
+D_TILES = D // P
+LO = 32
+HI = HW // LO
+PHI_BUFS = 8
+G_BUFS = 3
+W_BUFS = 5
+A_BUFS = 2 * A_PASSES
+PSUM_BANKS = 8
+Z_COPIES = 16
+T_PER_CHUNK = N_TILE // COLS_PER_T
+J = N_TILE // P
+
+FLOPS = 2 * 2 * D * (2 * C) * N
+
+
+def tile_nlgate_pa_kernel(tc, v, a, Wp, bp, Wg, bg, out_0, out_1):
+    nc = tc.nc
+    with ExitStack() as ctx:
+        const = ctx.enter_context(tc.tile_pool(name="const", bufs=1))
+        keep = ctx.enter_context(tc.tile_pool(name="keep", bufs=1))
+        stage = ctx.enter_context(tc.tile_pool(name="stage", bufs=W_BUFS))
+        outs = ctx.enter_context(tc.tile_pool(name="outs", bufs=PHI_BUFS))
+        psum = ctx.enter_context(tc.psum_pool(name="psum", bufs=PSUM_BANKS))
+        ctx.enter_context(tc.manual_schedule())
+
+        bias_rows = const.tile([P, P], BF16)
+        nc.gpsimd.memset(bias_rows[:], 0.0)
+        nc.sync.dma_start(out=bias_rows[0:D_TILES, :], in_=bp.rearrange("(m p) -> m p", p=P))
+        nc.sync.dma_start(out=bias_rows[D_TILES : 2 * D_TILES, :], in_=bg.rearrange("(m p) -> m p", p=P))
+
+        v_slabs = v.rearrange("b (kp p u e) t h w -> p (b kp) u (e t h w)", kp=Z_PASSES, p=P, u=2, e=2)
+        v_raw = []
+        for s in range(SLABS):
+            v_slab = keep.tile([P, 2 * T * HW], BF16, name="v_raw%d" % s)
+            nc.sync.dma_start(out=v_slab[:], in_=v_slabs[:, s // 2, s % 2, :])
+            v_raw.append(v_slab)
+
+        w_raw = {}
+
+        def load_weight(label, w):
+            for half in range(2):
+                w_half = keep.tile([P, 2, 2 * C], BF16, name="w%s_raw%d" % (label, half))
+                nc.sync.dma_start(
+                    out=w_half[:],
+                    in_=w[2 * P * half : 2 * P * (half + 1), :].rearrange("(p m) k -> p m k", m=2),
+                )
+                w_raw[(label, half)] = w_half
+
+        a_slabs = a.rearrange("b (kp p u e) at af -> p (b kp) u e (at af)", kp=A_PASSES, p=P, u=2, e=2)
+        a_raw = []
+
+        def load_audio(c, chunks):
+            a_cols = keep.tile([P, SLABS, 2, N_TILE * chunks], BF16, name="a_raw%d" % c)
+            for s in range(SLABS):
+                nc.sync.dma_start(
+                    out=a_cols[:, s, :, :], in_=a_slabs[:, s // 2, s % 2, :, N_TILE * c : N_TILE * (c + chunks)]
+                )
+            for i in range(chunks):
+                a_raw.append(a_cols[:, :, :, N_TILE * i : N_TILE * (i + 1)])
+
+        load_weight("g", Wg)
+        load_audio(0, 1)
+        load_weight("p", Wp)
+        load_audio(1, 1)
+        load_audio(2, 2)
+
+        ident_bf16 = const.tile([P, P], BF16)
+        make_identity(nc, ident_bf16[:])
+        ident_f32 = const.tile([P, P], F32)
+        make_identity(nc, ident_f32[:])
+
+        bias_cols = const.tile([P, 2 * D_TILES], F32)
+        bp_cols = bias_cols[:, 0:D_TILES]
+        bg_all = const.tile([P, D], F32)
+
+        def spread_biases():
+            bias_flipped = psum.tile([P, P], BF16, tag="bank")
+            nc.tensor.transpose(bias_flipped[:], bias_rows[:], ident_bf16[:])
+            nc.vector.tensor_copy(out=bias_cols[:], in_=bias_flipped[:, 0 : 2 * D_TILES])
+            bg_wide = const.tile([P, D_TILES, P], F32)
+            nc.vector.tensor_copy(
+                out=bg_wide[:], in_=bias_cols[:, D_TILES : 2 * D_TILES].unsqueeze(2).to_broadcast([P, D_TILES, P])
+            )
+            bg_spread = psum.tile([P, D_TILES, P], F32, tag="bank")
+            for m in range(D_TILES):
+                nc.tensor.transpose(bg_spread[:, m, :], bg_wide[:, m, :], ident_f32[:])
+            nc.vector.tensor_copy(out=bg_all[:], in_=bg_spread[:].rearrange("p m d -> p (m d)"))
+
+        w_codes = {}
+        w_planes = {}
+        for label in ("g", "p"):
+            w_codes[label] = keep.tile([P, A_PASSES + Z_PASSES, D], U32, align_bytes=64, name="w%s_codes" % label)
+            w_planes[label] = keep.tile([P, A_PASSES + Z_PASSES, D], U8, align_bytes=64, name="w%s_planes" % label)
+
+        def quantise_weight_half(label, half):
+            words = w_raw[(label, half)][:].bitcast(F32)
+            d_cols = slice(2 * P * half, 2 * P * (half + 1))
+            for kp in range(A_PASSES + Z_PASSES):
+                flipped = psum.tile([P, 2, 2 * P], F32, tag="bank")
+                for u in range(2):
+                    for m in range(2):
+                        every_2nd = slice(2 * P * kp + u, 2 * P * (kp + 1), 2)
+                        nc.tensor.transpose(
+                            flipped[:, u, P * m : P * (m + 1)], words[:, m, every_2nd], ident_f32[:]
+                        )
+                w_grouped = stage.tile([P, 2 * P, 4], BF16, align_bytes=64)
+                nc.scalar.copy(
+                    out=w_grouped[:].bitcast(F32).rearrange("p (q m) u -> p q m u", m=2),
+                    in_=flipped[:].rearrange("p u (m q) -> p q m u", m=2),
+                )
+                nc.vector.quantize_mx(
+                    out=w_codes[label][:, kp, d_cols].bitcast(FP8X4),
+                    scales=w_planes[label][:, kp, d_cols],
+                    in_=w_grouped[:].rearrange("p d j -> p (d j)"),
+                )
+
+        z_sums = keep.tile([P, SLABS, 2 * T], F32)
+
+        def fold_video():
+            for s in range(SLABS):
+                frames = v_raw[s][:].rearrange("p (f hi lo) -> p hi f lo", hi=HI, lo=LO)
+                folded = psum.tile([P, 2 * T, LO], F32, tag="bank")
+                for hi in range(HI):
+                    nc.tensor.matmul(
+                        folded[:], lhsT=ident_bf16[:], rhs=frames[:, hi], start=(hi == 0), stop=(hi == HI - 1)
+                    )
+                nc.vector.tensor_reduce(out=z_sums[:, s, :], in_=folded[:], axis=mybir.AxisListType.X, op=ADD)
+
+        z_codes = keep.tile([P, Z_PASSES, T * Z_COPIES], U32, align_bytes=64)
+        z_planes = keep.tile([P, Z_PASSES, T * Z_COPIES], U8, align_bytes=64)
+        nc.vector.memset(z_planes[:].bitcast(I32), 0)
+        z_wide_codes = keep.tile([P, Z_PASSES * CHUNKS, P], U32, align_bytes=64)
+        z_wide_planes = keep.tile([P, Z_PASSES * CHUNKS, P], U8, align_bytes=64)
+
+        def quantise_video():
+            z_grouped = keep.tile([P, Z_PASSES, T, Z_COPIES, 4], BF16, align_bytes=64)
+            for kp in range(Z_PASSES):
+                nc.vector.tensor_scalar(
+                    out=z_grouped[:, kp],
+                    in0=z_sums[:, 2 * kp : 2 * kp + 2, :]
+                    .rearrange("p u (e t) -> p t (u e)", e=2)
+                    .unsqueeze(2)
+                    .to_broadcast([P, T, Z_COPIES, 4]),
+                    scalar1=1.0 / HW,
+                    scalar2=None,
+                    op0=MULT,
+                )
+            nc.vector.quantize_mx(
+                out=z_codes[:].rearrange("p kp c -> p (kp c)").bitcast(FP8X4),
+                scales=z_planes[:].rearrange("p kp c -> p (kp c)"),
+                in_=z_grouped[:].rearrange("p kp t r j -> p (kp t r j)"),
+            )
+            repeats = P // T_PER_CHUNK // Z_COPIES
+            nc.vector.tensor_copy(
+                out=z_wide_codes[:].bitcast(I32).rearrange("p s (i b r) -> p (s i) b r", i=T_PER_CHUNK, b=repeats),
+                in_=z_codes[:]
+                .bitcast(I32)
+                .rearrange("p kp (t r) -> p (kp t) r", t=T)
+                .unsqueeze(2)
+                .to_broadcast([P, Z_PASSES * T, repeats, Z_COPIES]),
+            )
+            nc.vector.tensor_copy(
+                out=z_wide_planes[:].bitcast(I32).rearrange("p s (i b r) -> p (s i) b r", i=T_PER_CHUNK, b=repeats),
+                in_=z_planes[:]
+                .bitcast(I32)
+                .rearrange("p kp (t r) -> p (kp t) r", t=T)
+                .unsqueeze(2)
+                .to_broadcast([P, Z_PASSES * T, repeats, Z_COPIES // 4]),
+            )
+
+        g_bias = keep.tile([P, CHUNKS, D], F32)
+
+        def video_rows_for_g(c):
+            z_g = psum.tile([P, D], F32, tag="bank")
+            for kp in range(Z_PASSES):
+                nc.tensor.matmul_mx(
+                    out=z_g[:],
+                    lhsT=z_wide_codes[:, CHUNKS * kp + c, :].bitcast(FP8X4),
+                    lhsT_scale=z_wide_planes[:, CHUNKS * kp + c, :],
+                    rhs=w_codes["g"][:, A_PASSES + kp, :].bitcast(FP8X4),
+                    rhs_scale=w_planes["g"][:, A_PASSES + kp, :],
+                    start=(kp == 0),
+                    stop=(kp == Z_PASSES - 1),
+                )
+            nc.vector.tensor_tensor(out=g_bias[:, c, :], in0=z_g[:], in1=bg_all[:], op=ADD)
+
+        phi_bias = keep.tile([P, D_TILES, T], F32)
+
+        def video_columns_for_phi():
+            z_phi = psum.tile([P, D_TILES, T, Z_COPIES], F32, tag="bank")
+            for m in range(D_TILES):
+                for kp in range(Z_PASSES):
+                    nc.tensor.matmul_mx(
+                        out=z_phi[:, m],
+                        lhsT=w_codes["p"][:, A_PASSES + kp, P * m : P * (m + 1)].bitcast(FP8X4),
+                        lhsT_scale=w_planes["p"][:, A_PASSES + kp, P * m : P * (m + 1)],
+                        rhs=z_codes[:, kp, :].bitcast(FP8X4),
+                        rhs_scale=z_planes[:, kp, :],
+                        start=(kp == 0),
+                        stop=(kp == Z_PASSES - 1),
+                    )
+            nc.vector.tensor_tensor(
+                out=phi_bias[:],
+                in0=z_phi[:, :, :, 0],
+                in1=bp_cols.unsqueeze(2).to_broadcast([P, D_TILES, T]),
+                op=ADD,
+            )
+
+        a_codes = keep.tile([P, A_PASSES, N], U32, align_bytes=64)
+        a_planes = keep.tile([P, A_PASSES, N], U8, align_bytes=64)
+
+        def regroup_audio(c):
+            grouped = []
+            for kp in range(A_PASSES):
+                channels = a_raw[c][:, 2 * kp : 2 * kp + 2, :, :].rearrange("p u e (q j) -> p q (u e) j", j=J)
+                a_grouped = stage.tile([P, N_TILE, 4], BF16, align_bytes=64, bufs=A_BUFS)
+                spread = a_grouped[:].rearrange("p (j q) w -> p q w j", j=J)
+                if kp == 0 or c == 0:
+                    nc.vector.tensor_copy(out=spread, in_=channels)
+                else:
+                    nc.scalar.copy(out=spread, in_=channels)
+                grouped.append(a_grouped)
+            return grouped
+
+        def quantise_audio(c, grouped):
+            n_cols = slice(N_TILE * c, N_TILE * (c + 1))
+            for kp in range(A_PASSES):
+                nc.vector.quantize_mx(
+                    out=a_codes[:, kp, n_cols].bitcast(FP8X4),
+                    scales=a_planes[:, kp, n_cols],
+                    in_=grouped[kp][:].rearrange("p n w -> p (n w)"),
+                )
+
+        def g_tiles(c):
+            out_rows = out_1[0, N_TILE * c : N_TILE * (c + 1), :].rearrange("(q j) d -> q j d", j=J)
+            g_out = outs.tile([P, J, D], F32, bufs=G_BUFS)
+            for j in range(J):
+                places = slice(N_TILE * c + P * j, N_TILE * c + P * (j + 1))
+                g_acc = psum.tile([P, D], F32, tag="bank")
+                for kp in range(A_PASSES):
+                    nc.tensor.matmul_mx(
+                        out=g_acc[:],
+                        lhsT=a_codes[:, kp, places].bitcast(FP8X4),
+                        lhsT_scale=a_planes[:, kp, places],
+                        rhs=w_codes["g"][:, kp, :].bitcast(FP8X4),
+                        rhs_scale=w_planes["g"][:, kp, :],
+                        start=(kp == 0),
+                        stop=(kp == A_PASSES - 1),
+                    )
+                nc.vector.tensor_tensor(out=g_out[:, j, :], in0=g_acc[:], in1=g_bias[:, c, :], op=ADD)
+                if j % 2 == 1:
+                    nc.sync.dma_start(out=out_rows[:, j - 1 : j + 1, :], in_=g_out[:, j - 1 : j + 1, :])
+
+        def phi_tile(c, m):
+            n_cols = slice(N_TILE * c, N_TILE * (c + 1))
+            d_rows = slice(P * m, P * (m + 1))
+            phi_acc = psum.tile([P, N_TILE], F32, tag="bank")
+            for kp in range(A_PASSES):
+                nc.tensor.matmul_mx(
+                    out=phi_acc[:],
+                    lhsT=w_codes["p"][:, kp, d_rows].bitcast(FP8X4),
+                    lhsT_scale=w_planes["p"][:, kp, d_rows],
+                    rhs=a_codes[:, kp, n_cols].bitcast(FP8X4),
+                    rhs_scale=a_planes[:, kp, n_cols],
+                    start=(kp == 0),
+                    stop=(kp == A_PASSES - 1),
+                )
+            by_column = phi_acc[:].rearrange("p (j i x) -> p i x j", j=J, i=T_PER_CHUNK)
+            phi_out = outs.tile([P, T_PER_CHUNK, COLS_PER_T // J, J], F32)
+            for i in range(T_PER_CHUNK):
+                t = T_PER_CHUNK * c + i
+                nc.scalar.activation(
+                    out=phi_out[:, i], in_=by_column[:, i], func=IDENTITY, bias=phi_bias[:, m, t : t + 1]
+                )
+            nc.sync.dma_start(out=out_0[0, d_rows, n_cols], in_=phi_out[:].rearrange("p i x j -> p (i x j)"))
+
+        spread_biases()
+        fold_video()
+        quantise_video()
+        quantise_weight_half("g", 0)
+        quantise_weight_half("g", 1)
+        grouped = regroup_audio(0)
+        quantise_audio(0, grouped)
+        quantise_weight_half("p", 0)
+        quantise_weight_half("p", 1)
+        video_rows_for_g(0)
+        for c in range(CHUNKS):
+            if c + 1 < CHUNKS:
+                grouped = regroup_audio(c + 1)
+            g_tiles(c)
+            if c + 1 < CHUNKS:
+                quantise_audio(c + 1, grouped)
+                video_rows_for_g(c + 1)
+            if c == 0:
+                video_columns_for_phi()
+            for m in range(D_TILES):
+                phi_tile(c, m)

@@ -11,6 +11,7 @@ U8 = mybir.dt.uint8
 FP8X4 = mybir.dt.float8_e4m3fn_x4
 ADD = mybir.AluOpType.add
 MULT = mybir.AluOpType.mult
+COPY = mybir.ActivationFunctionType.Copy
 IDENTITY = mybir.ActivationFunctionType.Identity
 
 P = 128
@@ -31,7 +32,7 @@ LO = 32
 HI = HW // LO
 PHI_BUFS = 8
 G_BUFS = 3
-W_BUFS = 5
+W_BUFS = 8
 A_BUFS = 2 * A_PASSES
 PSUM_BANKS = 8
 Z_COPIES = 16
@@ -56,41 +57,49 @@ def tile_nlgate_pa_kernel(tc, v, a, Wp, bp, Wg, bg, out_0, out_1):
         nc.sync.dma_start(out=bias_rows[0:D_TILES, :], in_=bp.rearrange("(m p) -> m p", p=P))
         nc.sync.dma_start(out=bias_rows[D_TILES : 2 * D_TILES, :], in_=bg.rearrange("(m p) -> m p", p=P))
 
+        w_raw = {}
+
+        def load_weight(label, w, half):
+            w_half = keep.tile([P, 2, 2 * C], BF16, name="w%s_raw%d" % (label, half))
+            nc.sync.dma_start(
+                out=w_half[:],
+                in_=w[2 * P * half : 2 * P * (half + 1), :].rearrange("(p m) k -> p m k", m=2),
+            )
+            w_raw[(label, half)] = w_half
+
+        a_view = a.rearrange("b (kp p w) at af -> p (b kp) w (at af)", kp=A_PASSES, p=P, w=4)
+        a_raw = {}
+
+        def load_audio(kp, c, chunks):
+            a_cols = keep.tile([P, 4, N_TILE * chunks], BF16, name="a_raw%d_%d" % (kp, c))
+            nc.sync.dma_start(out=a_cols[:], in_=a_view[:, kp, :, N_TILE * c : N_TILE * (c + chunks)])
+            for i in range(chunks):
+                a_raw[(c + i, kp)] = a_cols[:, :, N_TILE * i : N_TILE * (i + 1)]
+
+
         v_slabs = v.rearrange("b (kp p u e) t h w -> p (b kp) u (e t h w)", kp=Z_PASSES, p=P, u=2, e=2)
         v_raw = []
-        for s in range(SLABS):
+
+        def load_video(s):
             v_slab = keep.tile([P, 2 * T * HW], BF16, name="v_raw%d" % s)
             nc.sync.dma_start(out=v_slab[:], in_=v_slabs[:, s // 2, s % 2, :])
             v_raw.append(v_slab)
 
-        w_raw = {}
 
-        def load_weight(label, w):
-            for half in range(2):
-                w_half = keep.tile([P, 2, 2 * C], BF16, name="w%s_raw%d" % (label, half))
-                nc.sync.dma_start(
-                    out=w_half[:],
-                    in_=w[2 * P * half : 2 * P * (half + 1), :].rearrange("(p m) k -> p m k", m=2),
-                )
-                w_raw[(label, half)] = w_half
-
-        a_slabs = a.rearrange("b (kp p u e) at af -> p (b kp) u e (at af)", kp=A_PASSES, p=P, u=2, e=2)
-        a_raw = []
-
-        def load_audio(c, chunks):
-            a_cols = keep.tile([P, SLABS, 2, N_TILE * chunks], BF16, name="a_raw%d" % c)
-            for s in range(SLABS):
-                nc.sync.dma_start(
-                    out=a_cols[:, s, :, :], in_=a_slabs[:, s // 2, s % 2, :, N_TILE * c : N_TILE * (c + chunks)]
-                )
-            for i in range(chunks):
-                a_raw.append(a_cols[:, :, :, N_TILE * i : N_TILE * (i + 1)])
-
-        load_weight("g", Wg)
-        load_audio(0, 1)
-        load_weight("p", Wp)
-        load_audio(1, 1)
-        load_audio(2, 2)
+        load_video(0)
+        load_video(1)
+        load_video(2)
+        load_video(3)
+        load_weight("g", Wg, 0)
+        load_weight("g", Wg, 1)
+        load_audio(0, 0, 1)
+        load_audio(1, 0, 1)
+        load_weight("p", Wp, 0)
+        load_weight("p", Wp, 1)
+        load_audio(0, 1, 1)
+        load_audio(1, 1, 1)
+        load_audio(0, 2, 2)
+        load_audio(1, 2, 2)
 
         ident_bf16 = const.tile([P, P], BF16)
         make_identity(nc, ident_bf16[:])
@@ -120,39 +129,40 @@ def tile_nlgate_pa_kernel(tc, v, a, Wp, bp, Wg, bg, out_0, out_1):
             w_codes[label] = keep.tile([P, A_PASSES + Z_PASSES, D], U32, align_bytes=64, name="w%s_codes" % label)
             w_planes[label] = keep.tile([P, A_PASSES + Z_PASSES, D], U8, align_bytes=64, name="w%s_planes" % label)
 
-        def quantise_weight_half(label, half):
-            words = w_raw[(label, half)][:].bitcast(F32)
+        def flip_weight(label, half, kp):
+            words = w_raw[(label, half)][:].bitcast(F32).rearrange("p m (k q u) -> p m k u q", q=P, u=2)
+            flipped = psum.tile([P, 2, 2 * P], F32, tag="bank")
+            for u in range(2):
+                for m in range(2):
+                    nc.tensor.transpose(flipped[:, u, P * m : P * (m + 1)], words[:, m, kp, u, :], ident_f32[:])
+            w_grouped = stage.tile([P, 2 * P, 4], BF16, align_bytes=64)
+            nc.scalar.copy(
+                out=w_grouped[:].bitcast(F32).rearrange("p (q m) u -> p q m u", m=2),
+                in_=flipped[:].rearrange("p u (m q) -> p q m u", m=2),
+            )
+            return w_grouped
+
+        def quantise_weight(label, half, kp, w_grouped):
             d_cols = slice(2 * P * half, 2 * P * (half + 1))
-            for kp in range(A_PASSES + Z_PASSES):
-                flipped = psum.tile([P, 2, 2 * P], F32, tag="bank")
-                for u in range(2):
-                    for m in range(2):
-                        every_2nd = slice(2 * P * kp + u, 2 * P * (kp + 1), 2)
-                        nc.tensor.transpose(
-                            flipped[:, u, P * m : P * (m + 1)], words[:, m, every_2nd], ident_f32[:]
-                        )
-                w_grouped = stage.tile([P, 2 * P, 4], BF16, align_bytes=64)
-                nc.scalar.copy(
-                    out=w_grouped[:].bitcast(F32).rearrange("p (q m) u -> p q m u", m=2),
-                    in_=flipped[:].rearrange("p u (m q) -> p q m u", m=2),
-                )
-                nc.vector.quantize_mx(
-                    out=w_codes[label][:, kp, d_cols].bitcast(FP8X4),
-                    scales=w_planes[label][:, kp, d_cols],
-                    in_=w_grouped[:].rearrange("p d j -> p (d j)"),
-                )
+            nc.vector.quantize_mx(
+                out=w_codes[label][:, kp, d_cols].bitcast(FP8X4),
+                scales=w_planes[label][:, kp, d_cols],
+                in_=w_grouped[:].rearrange("p d j -> p (d j)"),
+            )
 
         z_sums = keep.tile([P, SLABS, 2 * T], F32)
 
-        def fold_video():
-            for s in range(SLABS):
-                frames = v_raw[s][:].rearrange("p (f hi lo) -> p hi f lo", hi=HI, lo=LO)
-                folded = psum.tile([P, 2 * T, LO], F32, tag="bank")
-                for hi in range(HI):
-                    nc.tensor.matmul(
-                        folded[:], lhsT=ident_bf16[:], rhs=frames[:, hi], start=(hi == 0), stop=(hi == HI - 1)
-                    )
-                nc.vector.tensor_reduce(out=z_sums[:, s, :], in_=folded[:], axis=mybir.AxisListType.X, op=ADD)
+        def fold_slab(s):
+            frames = v_raw[s][:].rearrange("p (f hi lo) -> p hi f lo", hi=HI, lo=LO)
+            folded = psum.tile([P, 2 * T, LO], F32, tag="bank")
+            for hi in range(HI):
+                nc.tensor.matmul(
+                    folded[:], lhsT=ident_bf16[:], rhs=frames[:, hi], start=(hi == 0), stop=(hi == HI - 1)
+                )
+            return folded
+
+        def finish_fold(s, folded):
+            nc.vector.tensor_reduce(out=z_sums[:, s, :], in_=folded[:], axis=mybir.AxisListType.X, op=ADD)
 
         z_codes = keep.tile([P, Z_PASSES, T * Z_COPIES], U32, align_bytes=64)
         z_planes = keep.tile([P, Z_PASSES, T * Z_COPIES], U8, align_bytes=64)
@@ -160,41 +170,42 @@ def tile_nlgate_pa_kernel(tc, v, a, Wp, bp, Wg, bg, out_0, out_1):
         z_wide_codes = keep.tile([P, Z_PASSES * CHUNKS, P], U32, align_bytes=64)
         z_wide_planes = keep.tile([P, Z_PASSES * CHUNKS, P], U8, align_bytes=64)
 
+        z_grouped = keep.tile([P, Z_PASSES, T, Z_COPIES, 4], BF16, align_bytes=64)
+
+        def scale_video(kp, engine="scalar"):
+            sums = (
+                z_sums[:, 2 * kp : 2 * kp + 2, :]
+                .rearrange("p u (e t) -> p t (u e)", e=2)
+                .unsqueeze(2)
+                .to_broadcast([P, T, Z_COPIES, 4])
+            )
+            if engine == "scalar":
+                nc.scalar.activation(out=z_grouped[:, kp], in_=sums, func=COPY, scale=1.0 / HW)
+            else:
+                nc.vector.tensor_scalar(out=z_grouped[:, kp], in0=sums, scalar1=1.0 / HW, scalar2=None, op0=MULT)
+
         def quantise_video():
-            z_grouped = keep.tile([P, Z_PASSES, T, Z_COPIES, 4], BF16, align_bytes=64)
-            for kp in range(Z_PASSES):
-                nc.vector.tensor_scalar(
-                    out=z_grouped[:, kp],
-                    in0=z_sums[:, 2 * kp : 2 * kp + 2, :]
-                    .rearrange("p u (e t) -> p t (u e)", e=2)
-                    .unsqueeze(2)
-                    .to_broadcast([P, T, Z_COPIES, 4]),
-                    scalar1=1.0 / HW,
-                    scalar2=None,
-                    op0=MULT,
-                )
             nc.vector.quantize_mx(
                 out=z_codes[:].rearrange("p kp c -> p (kp c)").bitcast(FP8X4),
                 scales=z_planes[:].rearrange("p kp c -> p (kp c)"),
                 in_=z_grouped[:].rearrange("p kp t r j -> p (kp t r j)"),
             )
+
+        def widen_video(chunks):
             repeats = P // T_PER_CHUNK // Z_COPIES
-            nc.vector.tensor_copy(
-                out=z_wide_codes[:].bitcast(I32).rearrange("p s (i b r) -> p (s i) b r", i=T_PER_CHUNK, b=repeats),
-                in_=z_codes[:]
-                .bitcast(I32)
-                .rearrange("p kp (t r) -> p (kp t) r", t=T)
-                .unsqueeze(2)
-                .to_broadcast([P, Z_PASSES * T, repeats, Z_COPIES]),
-            )
-            nc.vector.tensor_copy(
-                out=z_wide_planes[:].bitcast(I32).rearrange("p s (i b r) -> p (s i) b r", i=T_PER_CHUNK, b=repeats),
-                in_=z_planes[:]
-                .bitcast(I32)
-                .rearrange("p kp (t r) -> p (kp t) r", t=T)
-                .unsqueeze(2)
-                .to_broadcast([P, Z_PASSES * T, repeats, Z_COPIES // 4]),
-            )
+            ts = slice(T_PER_CHUNK * chunks[0], T_PER_CHUNK * (chunks[-1] + 1))
+            n = T_PER_CHUNK * len(chunks)
+            for wide, narrow, run in ((z_wide_codes, z_codes, Z_COPIES), (z_wide_planes, z_planes, Z_COPIES // 4)):
+                nc.vector.tensor_copy(
+                    out=wide[:]
+                    .bitcast(I32)
+                    .rearrange("p (kp c) (i b r) -> p kp (c i) b r", kp=Z_PASSES, i=T_PER_CHUNK, b=repeats)[:, :, ts],
+                    in_=narrow[:]
+                    .bitcast(I32)
+                    .rearrange("p kp (t r) -> p kp t r", t=T)[:, :, ts]
+                    .unsqueeze(3)
+                    .to_broadcast([P, Z_PASSES, n, repeats, run]),
+                )
 
         g_bias = keep.tile([P, CHUNKS, D], F32)
 
@@ -210,74 +221,87 @@ def tile_nlgate_pa_kernel(tc, v, a, Wp, bp, Wg, bg, out_0, out_1):
                     start=(kp == 0),
                     stop=(kp == Z_PASSES - 1),
                 )
+            return z_g
+
+        def join_bias_for_g(c, z_g):
             nc.vector.tensor_tensor(out=g_bias[:, c, :], in0=z_g[:], in1=bg_all[:], op=ADD)
 
         phi_bias = keep.tile([P, D_TILES, T], F32)
 
-        def video_columns_for_phi():
-            z_phi = psum.tile([P, D_TILES, T, Z_COPIES], F32, tag="bank")
-            for m in range(D_TILES):
+        def video_columns_for_phi(half):
+            z_phi = psum.tile([P, 2, T, Z_COPIES], F32, tag="bank")
+            for i in range(2):
+                m_cols = slice(P * (2 * half + i), P * (2 * half + i + 1))
                 for kp in range(Z_PASSES):
                     nc.tensor.matmul_mx(
-                        out=z_phi[:, m],
-                        lhsT=w_codes["p"][:, A_PASSES + kp, P * m : P * (m + 1)].bitcast(FP8X4),
-                        lhsT_scale=w_planes["p"][:, A_PASSES + kp, P * m : P * (m + 1)],
+                        out=z_phi[:, i],
+                        lhsT=w_codes["p"][:, A_PASSES + kp, m_cols].bitcast(FP8X4),
+                        lhsT_scale=w_planes["p"][:, A_PASSES + kp, m_cols],
                         rhs=z_codes[:, kp, :].bitcast(FP8X4),
                         rhs_scale=z_planes[:, kp, :],
                         start=(kp == 0),
                         stop=(kp == Z_PASSES - 1),
                     )
+            return z_phi
+
+        def join_bias_for_phi(half, z_phi):
+            ms = slice(2 * half, 2 * half + 2)
             nc.vector.tensor_tensor(
-                out=phi_bias[:],
+                out=phi_bias[:, ms, :],
                 in0=z_phi[:, :, :, 0],
-                in1=bp_cols.unsqueeze(2).to_broadcast([P, D_TILES, T]),
+                in1=bp_cols[:, ms].unsqueeze(2).to_broadcast([P, 2, T]),
                 op=ADD,
             )
 
         a_codes = keep.tile([P, A_PASSES, N], U32, align_bytes=64)
         a_planes = keep.tile([P, A_PASSES, N], U8, align_bytes=64)
 
-        def regroup_audio(c):
-            grouped = []
-            for kp in range(A_PASSES):
-                channels = a_raw[c][:, 2 * kp : 2 * kp + 2, :, :].rearrange("p u e (q j) -> p q (u e) j", j=J)
-                a_grouped = stage.tile([P, N_TILE, 4], BF16, align_bytes=64, bufs=A_BUFS)
-                spread = a_grouped[:].rearrange("p (j q) w -> p q w j", j=J)
-                if kp == 0 or c == 0:
-                    nc.vector.tensor_copy(out=spread, in_=channels)
-                else:
-                    nc.scalar.copy(out=spread, in_=channels)
-                grouped.append(a_grouped)
-            return grouped
+        def regroup_audio(c, kp, engine):
+            channels = a_raw[(c, kp)].rearrange("p w (q j) -> p q w j", j=J)
+            a_grouped = stage.tile([P, N_TILE, 4], BF16, align_bytes=64, bufs=A_BUFS)
+            spread = a_grouped[:].rearrange("p (j q) w -> p q w j", j=J)
+            if engine == "vector":
+                nc.vector.tensor_copy(out=spread, in_=channels)
+            else:
+                nc.scalar.copy(out=spread, in_=channels)
+            return a_grouped
 
-        def quantise_audio(c, grouped):
+        def quantise_audio(c, kp, a_grouped):
             n_cols = slice(N_TILE * c, N_TILE * (c + 1))
-            for kp in range(A_PASSES):
-                nc.vector.quantize_mx(
-                    out=a_codes[:, kp, n_cols].bitcast(FP8X4),
-                    scales=a_planes[:, kp, n_cols],
-                    in_=grouped[kp][:].rearrange("p n w -> p (n w)"),
-                )
+            nc.vector.quantize_mx(
+                out=a_codes[:, kp, n_cols].bitcast(FP8X4),
+                scales=a_planes[:, kp, n_cols],
+                in_=a_grouped[:].rearrange("p n w -> p (n w)"),
+            )
 
-        def g_tiles(c):
-            out_rows = out_1[0, N_TILE * c : N_TILE * (c + 1), :].rearrange("(q j) d -> q j d", j=J)
-            g_out = outs.tile([P, J, D], F32, bufs=G_BUFS)
-            for j in range(J):
-                places = slice(N_TILE * c + P * j, N_TILE * c + P * (j + 1))
-                g_acc = psum.tile([P, D], F32, tag="bank")
-                for kp in range(A_PASSES):
-                    nc.tensor.matmul_mx(
-                        out=g_acc[:],
-                        lhsT=a_codes[:, kp, places].bitcast(FP8X4),
-                        lhsT_scale=a_planes[:, kp, places],
-                        rhs=w_codes["g"][:, kp, :].bitcast(FP8X4),
-                        rhs_scale=w_planes["g"][:, kp, :],
-                        start=(kp == 0),
-                        stop=(kp == A_PASSES - 1),
-                    )
-                nc.vector.tensor_tensor(out=g_out[:, j, :], in0=g_acc[:], in1=g_bias[:, c, :], op=ADD)
-                if j % 2 == 1:
-                    nc.sync.dma_start(out=out_rows[:, j - 1 : j + 1, :], in_=g_out[:, j - 1 : j + 1, :])
+        g_outs = {}
+
+        def g_product(c, j):
+            places = slice(N_TILE * c + P * j, N_TILE * c + P * (j + 1))
+            g_acc = psum.tile([P, D], F32, tag="bank")
+            for kp in range(A_PASSES):
+                nc.tensor.matmul_mx(
+                    out=g_acc[:],
+                    lhsT=a_codes[:, kp, places].bitcast(FP8X4),
+                    lhsT_scale=a_planes[:, kp, places],
+                    rhs=w_codes["g"][:, kp, :].bitcast(FP8X4),
+                    rhs_scale=w_planes["g"][:, kp, :],
+                    start=(kp == 0),
+                    stop=(kp == A_PASSES - 1),
+                )
+            return g_acc
+
+        def g_finish(c, j, g_acc):
+            if j == 0:
+                g_outs[c] = outs.tile([P, J, D], F32, name="g_out", bufs=G_BUFS)
+            g_out = g_outs[c]
+            nc.vector.tensor_tensor(out=g_out[:, j, :], in0=g_acc[:], in1=g_bias[:, c, :], op=ADD)
+            if j % 2 == 1:
+                out_rows = out_1[0, N_TILE * c : N_TILE * (c + 1), :].rearrange("(q j) d -> q j d", j=J)
+                nc.sync.dma_start(out=out_rows[:, j - 1 : j + 1, :], in_=g_out[:, j - 1 : j + 1, :])
+
+        def g_tile(c, j):
+            g_finish(c, j, g_product(c, j))
 
         def phi_tile(c, m):
             n_cols = slice(N_TILE * c, N_TILE * (c + 1))
@@ -302,24 +326,50 @@ def tile_nlgate_pa_kernel(tc, v, a, Wp, bp, Wg, bg, out_0, out_1):
                 )
             nc.sync.dma_start(out=out_0[0, d_rows, n_cols], in_=phi_out[:].rearrange("p i x j -> p (i x j)"))
 
+        passes = range(A_PASSES + Z_PASSES)
         spread_biases()
-        fold_video()
+        for kp in range(Z_PASSES):
+            for s in (2 * kp, 2 * kp + 1):
+                finish_fold(s, fold_slab(s))
+            scale_video(kp, "vector")
         quantise_video()
-        quantise_weight_half("g", 0)
-        quantise_weight_half("g", 1)
-        grouped = regroup_audio(0)
-        quantise_audio(0, grouped)
-        quantise_weight_half("p", 0)
-        quantise_weight_half("p", 1)
-        video_rows_for_g(0)
+        widen_video([0])
+        for kp in passes:
+            quantise_weight("g", 0, kp, flip_weight("g", 0, kp))
+        flipped = [flip_weight("g", 1, kp) for kp in passes]
+        grouped = [regroup_audio(0, 0, "vector"), regroup_audio(0, 1, "scalar")]
+        for kp in passes:
+            quantise_weight("g", 1, kp, flipped[kp])
+        quantise_audio(0, 0, grouped[0])
+        flipped = [flip_weight("p", 0, kp) for kp in passes]
+        quantise_audio(0, 1, grouped[1])
+        widen_video([1, 2, 3])
+        for kp in passes:
+            quantise_weight("p", 0, kp, flipped[kp])
+        flipped = [flip_weight("p", 1, kp) for kp in passes]
+        z_g = video_rows_for_g(0)
+        for kp in passes:
+            quantise_weight("p", 1, kp, flipped[kp])
+        z_phi = [video_columns_for_phi(half) for half in range(2)]
+        join_bias_for_g(0, z_g)
+        for half in range(2):
+            join_bias_for_phi(half, z_phi[half])
         for c in range(CHUNKS):
             if c + 1 < CHUNKS:
-                grouped = regroup_audio(c + 1)
-            g_tiles(c)
-            if c + 1 < CHUNKS:
-                quantise_audio(c + 1, grouped)
-                video_rows_for_g(c + 1)
-            if c == 0:
-                video_columns_for_phi()
-            for m in range(D_TILES):
-                phi_tile(c, m)
+                grouped = [regroup_audio(c + 1, 0, "vector"), regroup_audio(c + 1, 1, "scalar")]
+                g_tile(c, 0)
+                phi_tile(c, 0)
+                quantise_audio(c + 1, 0, grouped[0])
+                phi_tile(c, 1)
+                g_tile(c, 1)
+                phi_tile(c, 2)
+                quantise_audio(c + 1, 1, grouped[1])
+                phi_tile(c, 3)
+                g_tile(c, 2)
+                g_tile(c, 3)
+                z_g = video_rows_for_g(c + 1)
+                join_bias_for_g(c + 1, z_g)
+            else:
+                for i in range(4):
+                    phi_tile(c, i)
+                    g_tile(c, i)

@@ -296,9 +296,10 @@ def tile_nlgate_pa_kernel(tc, v, a, Wp, bp, Wg, bg, out_0, out_1):
                 g_outs[c] = outs.tile([P, J, D], F32, name="g_out", bufs=G_BUFS)
             g_out = g_outs[c]
             nc.vector.tensor_tensor(out=g_out[:, j, :], in0=g_acc[:], in1=g_bias[:, c, :], op=ADD)
-            if j % 2 == 1:
-                out_rows = out_1[0, N_TILE * c : N_TILE * (c + 1), :].rearrange("(q j) d -> q j d", j=J)
-                nc.sync.dma_start(out=out_rows[:, j - 1 : j + 1, :], in_=g_out[:, j - 1 : j + 1, :])
+
+        def store_g(c, js):
+            out_rows = out_1[0, N_TILE * c : N_TILE * (c + 1), :].rearrange("(q j) d -> q j d", j=J)
+            nc.sync.dma_start(out=out_rows[:, js, :], in_=g_outs[c][:, js, :])
 
         def g_tile(c, j):
             g_finish(c, j, g_product(c, j))
@@ -356,7 +357,8 @@ def tile_nlgate_pa_kernel(tc, v, a, Wp, bp, Wg, bg, out_0, out_1):
             join_bias_for_phi(half, z_phi[half])
         for c in range(CHUNKS):
             if c + 1 < CHUNKS:
-                grouped = [regroup_audio(c + 1, 0, "vector"), regroup_audio(c + 1, 1, "scalar")]
+                grouped = [regroup_audio(c + 1, 0, "vector"), None]
+                grouped[1] = regroup_audio(c + 1, 1, "scalar")
                 g_tile(c, 0)
                 phi_tile(c, 0)
                 quantise_audio(c + 1, 0, grouped[0])
@@ -367,9 +369,17 @@ def tile_nlgate_pa_kernel(tc, v, a, Wp, bp, Wg, bg, out_0, out_1):
                 phi_tile(c, 3)
                 g_tile(c, 2)
                 g_tile(c, 3)
-                z_g = video_rows_for_g(c + 1)
-                join_bias_for_g(c + 1, z_g)
+                store_g(c, slice(0, 2))
+                store_g(c, slice(2, 4))
+                join_bias_for_g(c + 1, video_rows_for_g(c + 1))
             else:
-                for i in range(4):
-                    phi_tile(c, i)
-                    g_tile(c, i)
+                phi_tile(c, 0)
+                g_tile(c, 0)
+                phi_tile(c, 1)
+                g_tile(c, 1)
+                store_g(c, slice(0, 2))
+                phi_tile(c, 2)
+                g_tile(c, 2)
+                phi_tile(c, 3)
+                g_tile(c, 3)
+                store_g(c, slice(2, 4))

@@ -86,11 +86,11 @@ def tile_nlgate_pa_kernel(tc, v, a, Wp, bp, Wg, bg, out_0, out_1):
             v_raw.append(v_slab)
 
 
+        load_weight("g", Wg, 0)
         load_video(0)
         load_video(1)
         load_video(2)
         load_video(3)
-        load_weight("g", Wg, 0)
         load_weight("g", Wg, 1)
         load_audio(0, 0, 1)
         load_audio(1, 0, 1)
@@ -329,14 +329,14 @@ def tile_nlgate_pa_kernel(tc, v, a, Wp, bp, Wg, bg, out_0, out_1):
 
         passes = range(A_PASSES + Z_PASSES)
         spread_biases()
+        for kp in passes:
+            quantise_weight("g", 0, kp, flip_weight("g", 0, kp))
         for kp in range(Z_PASSES):
             for s in (2 * kp, 2 * kp + 1):
                 finish_fold(s, fold_slab(s))
             scale_video(kp, "vector")
         quantise_video()
         widen_video([0])
-        for kp in passes:
-            quantise_weight("g", 0, kp, flip_weight("g", 0, kp))
         flipped = [flip_weight("g", 1, kp) for kp in passes]
         grouped = [regroup_audio(0, 0, "vector"), regroup_audio(0, 1, "scalar")]
         for kp in passes:

@@ -262,8 +262,12 @@ def tile_nlgate_pa_kernel(tc, v, a, Wp, bp, Wg, bg, out_0, out_1):
             spread = a_grouped[:].rearrange("p (j q) w -> p q w j", j=J)
             if engine == "vector":
                 nc.vector.tensor_copy(out=spread, in_=channels)
-            else:
+            elif engine == "scalar":
                 nc.scalar.copy(out=spread, in_=channels)
+            else:
+                nc.gpsimd.tensor_scalar(
+                    out=spread, in0=channels, scalar1=1.0, scalar2=0.0, op0=MULT, op1=ADD
+                )
             return a_grouped
 
         def quantise_audio(c, kp, a_grouped):
@@ -357,8 +361,8 @@ def tile_nlgate_pa_kernel(tc, v, a, Wp, bp, Wg, bg, out_0, out_1):
             join_bias_for_phi(half, z_phi[half])
         for c in range(CHUNKS):
             if c + 1 < CHUNKS:
-                grouped = [regroup_audio(c + 1, 0, "vector"), None]
-                grouped[1] = regroup_audio(c + 1, 1, "scalar")
+                grouped = [regroup_audio(c + 1, 0, ("vector", "vector", "scalar")[c]), None]
+                grouped[1] = regroup_audio(c + 1, 1, ("scalar", "scalar", "gpsimd")[c])
                 g_tile(c, 0)
                 phi_tile(c, 0)
                 quantise_audio(c + 1, 0, grouped[0])

from contextlib import ExitStack

import concourse.mybir as mybir
from concourse.masks import make_identity

F32 = mybir.dt.float32
BF16 = mybir.dt.bfloat16
I32 = mybir.dt.int32
U32 = mybir.dt.uint32
U8 = mybir.dt.uint8
FP8X4 = mybir.dt.float8_e4m3fn_x4
ADD = mybir.AluOpType.add
MULT = mybir.AluOpType.mult
COPY = mybir.ActivationFunctionType.Copy
IDENTITY = mybir.ActivationFunctionType.Identity

P = 128
C = 1024
T = 8
HW = 256
N = 2048
COLS_PER_T = N // T
D = 512
K_PASS = 512
A_PASSES = C // K_PASS
Z_PASSES = C // K_PASS
SLABS = C // (2 * P)
N_TILE = 512
CHUNKS = N // N_TILE
D_TILES = D // P
LO = 32
HI = HW // LO
PHI_BUFS = 8
G_BUFS = 3
W_BUFS = 8
A_BUFS = 2 * A_PASSES
PSUM_BANKS = 8
Z_COPIES = 16
T_PER_CHUNK = N_TILE // COLS_PER_T
J = N_TILE // P

FLOPS = 2 * 2 * D * (2 * C) * N


def tile_nlgate_pa_kernel(tc, v, a, Wp, bp, Wg, bg, out_0, out_1):
    nc = tc.nc
    with ExitStack() as ctx:
        const = ctx.enter_context(tc.tile_pool(name="const", bufs=1))
        keep = ctx.enter_context(tc.tile_pool(name="keep", bufs=1))
        stage = ctx.enter_context(tc.tile_pool(name="stage", bufs=W_BUFS))
        outs = ctx.enter_context(tc.tile_pool(name="outs", bufs=PHI_BUFS))
        psum = ctx.enter_context(tc.psum_pool(name="psum", bufs=PSUM_BANKS))
        ctx.enter_context(tc.manual_schedule())

        bias_rows = const.tile([P, P], BF16)
        nc.gpsimd.memset(bias_rows[:], 0.0)
        nc.sync.dma_start(out=bias_rows[0:D_TILES, :], in_=bp.rearrange("(m p) -> m p", p=P))
        nc.sync.dma_start(out=bias_rows[D_TILES : 2 * D_TILES, :], in_=bg.rearrange("(m p) -> m p", p=P))

        w_raw = {}

        def load_weight(label, w, half):
            w_half = keep.tile([P, 2, 2 * C], BF16, name="w%s_raw%d" % (label, half))
            nc.sync.dma_start(
                out=w_half[:],
                in_=w[2 * P * half : 2 * P * (half + 1), :].rearrange("(p m) k -> p m k", m=2),
            )
            w_raw[(label, half)] = w_half

        a_view = a.rearrange("b (kp p w) at af -> p (b kp) w (at af)", kp=A_PASSES, p=P, w=4)
        a_raw = {}

        def load_audio(kp, c, chunks):
            a_cols = keep.tile([P, 4, N_TILE * chunks], BF16, name="a_raw%d_%d" % (kp, c))
            nc.sync.dma_start(out=a_cols[:], in_=a_view[:, kp, :, N_TILE * c : N_TILE * (c + chunks)])
            for i in range(chunks):
                a_raw[(c + i, kp)] = a_cols[:, :, N_TILE * i : N_TILE * (i + 1)]


        v_slabs = v.rearrange("b (kp p u e) t h w -> p (b kp) u (e t h w)", kp=Z_PASSES, p=P, u=2, e=2)
        v_raw = []

        def load_video(s):
            v_slab = keep.tile([P, 2 * T * HW], BF16, name="v_raw%d" % s)
            nc.sync.dma_start(out=v_slab[:], in_=v_slabs[:, s // 2, s % 2, :])
            v_raw.append(v_slab)


        load_weight("g", Wg, 0)
        load_video(0)
        load_video(1)
        load_video(2)
        load_video(3)
        load_weight("g", Wg, 1)
        load_audio(0, 0, 1)
        load_audio(1, 0, 1)
        load_weight("p", Wp, 0)
        load_weight("p", Wp, 1)
        load_audio(0, 1, 1)
        load_audio(1, 1, 1)
        load_audio(0, 2, 2)
        load_audio(1, 2, 2)

        ident_bf16 = const.tile([P, P], BF16)
        make_identity(nc, ident_bf16[:])
        ident_f32 = const.tile([P, P], F32)
        make_identity(nc, ident_f32[:])

        bias_cols = const.tile([P, 2 * D_TILES], F32)
        bp_cols = bias_cols[:, 0:D_TILES]
        bg_all = const.tile([P, D], F32)

        def spread_biases():
            bias_flipped = psum.tile([P, P], BF16, tag="bank")
            nc.tensor.transpose(bias_flipped[:], bias_rows[:], ident_bf16[:])
            nc.vector.tensor_copy(out=bias_cols[:], in_=bias_flipped[:, 0 : 2 * D_TILES])
            bg_wide = const.tile([P, D_TILES, P], F32)
            nc.vector.tensor_copy(
                out=bg_wide[:], in_=bias_cols[:, D_TILES : 2 * D_TILES].unsqueeze(2).to_broadcast([P, D_TILES, P])
            )
            bg_spread = psum.tile([P, D_TILES, P], F32, tag="bank")
            for m in range(D_TILES):
                nc.tensor.transpose(bg_spread[:, m, :], bg_wide[:, m, :], ident_f32[:])
            nc.vector.tensor_copy(out=bg_all[:], in_=bg_spread[:].rearrange("p m d -> p (m d)"))

        w_codes = {}
        w_planes = {}
        for label in ("g", "p"):
            w_codes[label] = keep.tile([P, A_PASSES + Z_PASSES, D], U32, align_bytes=64, name="w%s_codes" % label)
            w_planes[label] = keep.tile([P, A_PASSES + Z_PASSES, D], U8, align_bytes=64, name="w%s_planes" % label)

        def flip_weight(label, half, kp):
            words = w_raw[(label, half)][:].bitcast(F32).rearrange("p m (k q u) -> p m k u q", q=P, u=2)
            flipped = psum.tile([P, 2, 2 * P], F32, tag="bank")
            for u in range(2):
                for m in range(2):
                    nc.tensor.transpose(flipped[:, u, P * m : P * (m + 1)], words[:, m, kp, u, :], ident_f32[:])
            w_grouped = stage.tile([P, 2 * P, 4], BF16, align_bytes=64)
            nc.scalar.copy(
                out=w_grouped[:].bitcast(F32).rearrange("p (q m) u -> p q m u", m=2),
                in_=flipped[:].rearrange("p u (m q) -> p q m u", m=2),
            )
            return w_grouped

        def quantise_weight(label, half, kp, w_grouped):
            d_cols = slice(2 * P * half, 2 * P * (half + 1))
            nc.vector.quantize_mx(
                out=w_codes[label][:, kp, d_cols].bitcast(FP8X4),
                scales=w_planes[label][:, kp, d_cols],
                in_=w_grouped[:].rearrange("p d j -> p (d j)"),
            )

        z_sums = keep.tile([P, SLABS, 2 * T], F32)

        def fold_slab(s):
            frames = v_raw[s][:].rearrange("p (f hi lo) -> p hi f lo", hi=HI, lo=LO)
            folded = psum.tile([P, 2 * T, LO], F32, tag="bank")
            for hi in range(HI):
                nc.tensor.matmul(
                    folded[:], lhsT=ident_bf16[:], rhs=frames[:, hi], start=(hi == 0), stop=(hi == HI - 1)
                )
            return folded

        def finish_fold(s, folded):
            nc.vector.tensor_reduce(out=z_sums[:, s, :], in_=folded[:], axis=mybir.AxisListType.X, op=ADD)

        z_codes = keep.tile([P, Z_PASSES, T * Z_COPIES], U32, align_bytes=64)
        z_planes = keep.tile([P, Z_PASSES, T * Z_COPIES], U8, align_bytes=64)
        nc.vector.memset(z_planes[:].bitcast(I32), 0)
        z_wide_codes = keep.tile([P, Z_PASSES * CHUNKS, P], U32, align_bytes=64)
        z_wide_planes = keep.tile([P, Z_PASSES * CHUNKS, P], U8, align_bytes=64)

        z_grouped = keep.tile([P, Z_PASSES, T, Z_COPIES, 4], BF16, align_bytes=64)

        def scale_video(kp, engine="scalar"):
            sums = (
                z_sums[:, 2 * kp : 2 * kp + 2, :]
                .rearrange("p u (e t) -> p t (u e)", e=2)
                .unsqueeze(2)
                .to_broadcast([P, T, Z_COPIES, 4])
            )
            if engine == "scalar":
                nc.scalar.activation(out=z_grouped[:, kp], in_=sums, func=COPY, scale=1.0 / HW)
            else:
                nc.vector.tensor_scalar(out=z_grouped[:, kp], in0=sums, scalar1=1.0 / HW, scalar2=None, op0=MULT)

        def quantise_video():
            nc.vector.quantize_mx(
                out=z_codes[:].rearrange("p kp c -> p (kp c)").bitcast(FP8X4),
                scales=z_planes[:].rearrange("p kp c -> p (kp c)"),
                in_=z_grouped[:].rearrange("p kp t r j -> p (kp t r j)"),
            )

        def widen_video(chunks):
            repeats = P // T_PER_CHUNK // Z_COPIES
            ts = slice(T_PER_CHUNK * chunks[0], T_PER_CHUNK * (chunks[-1] + 1))
            n = T_PER_CHUNK * len(chunks)
            for wide, narrow, run in ((z_wide_codes, z_codes, Z_COPIES), (z_wide_planes, z_planes, Z_COPIES // 4)):
                nc.vector.tensor_copy(
                    out=wide[:]
                    .bitcast(I32)
                    .rearrange("p (kp c) (i b r) -> p kp (c i) b r", kp=Z_PASSES, i=T_PER_CHUNK, b=repeats)[:, :, ts],
                    in_=narrow[:]
                    .bitcast(I32)
                    .rearrange("p kp (t r) -> p kp t r", t=T)[:, :, ts]
                    .unsqueeze(3)
                    .to_broadcast([P, Z_PASSES, n, repeats, run]),
                )

        g_bias = keep.tile([P, CHUNKS, D], F32)

        def video_rows_for_g(c):
            z_g = psum.tile([P, D], F32, tag="bank")
            for kp in range(Z_PASSES):
                nc.tensor.matmul_mx(
                    out=z_g[:],
                    lhsT=z_wide_codes[:, CHUNKS * kp + c, :].bitcast(FP8X4),
                    lhsT_scale=z_wide_planes[:, CHUNKS * kp + c, :],
                    rhs=w_codes["g"][:, A_PASSES + kp, :].bitcast(FP8X4),
                    rhs_scale=w_planes["g"][:, A_PASSES + kp, :],
                    start=(kp == 0),
                    stop=(kp == Z_PASSES - 1),
                )
            return z_g

        def join_bias_for_g(c, z_g):
            nc.vector.tensor_tensor(out=g_bias[:, c, :], in0=z_g[:], in1=bg_all[:], op=ADD)

        phi_bias = keep.tile([P, D_TILES, T], F32)

        def video_columns_for_phi(half):
            z_phi = psum.tile([P, 2, T, Z_COPIES], F32, tag="bank")
            for i in range(2):
                m_cols = slice(P * (2 * half + i), P * (2 * half + i + 1))
                for kp in range(Z_PASSES):
                    nc.tensor.matmul_mx(
                        out=z_phi[:, i],
                        lhsT=w_codes["p"][:, A_PASSES + kp, m_cols].bitcast(FP8X4),
                        lhsT_scale=w_planes["p"][:, A_PASSES + kp, m_cols],
                        rhs=z_codes[:, kp, :].bitcast(FP8X4),
                        rhs_scale=z_planes[:, kp, :],
                        start=(kp == 0),
                        stop=(kp == Z_PASSES - 1),
                    )
            return z_phi

        def join_bias_for_phi(half, z_phi):
            ms = slice(2 * half, 2 * half + 2)
            nc.vector.tensor_tensor(
                out=phi_bias[:, ms, :],
                in0=z_phi[:, :, :, 0],
                in1=bp_cols[:, ms].unsqueeze(2).to_broadcast([P, 2, T]),
                op=ADD,
            )

        a_codes = keep.tile([P, A_PASSES, N], U32, align_bytes=64)
        a_planes = keep.tile([P, A_PASSES, N], U8, align_bytes=64)

        def regroup_audio(c, kp, engine):
            channels = a_raw[(c, kp)].rearrange("p w (q j) -> p q w j", j=J)
            a_grouped = stage.tile([P, N_TILE, 4], BF16, align_bytes=64, bufs=A_BUFS)
            spread = a_grouped[:].rearrange("p (j q) w -> p q w j", j=J)
            if engine == "vector":
                nc.vector.tensor_copy(out=spread, in_=channels)
            elif engine == "scalar":
                nc.scalar.copy(out=spread, in_=channels)
            else:
                nc.gpsimd.tensor_scalar(
                    out=spread, in0=channels, scalar1=1.0, scalar2=0.0, op0=MULT, op1=ADD
                )
            return a_grouped

        def quantise_audio(c, kp, a_grouped):
            n_cols = slice(N_TILE * c, N_TILE * (c + 1))
            nc.vector.quantize_mx(
                out=a_codes[:, kp, n_cols].bitcast(FP8X4),
                scales=a_planes[:, kp, n_cols],
                in_=a_grouped[:].rearrange("p n w -> p (n w)"),
            )

        g_outs = {}

        def g_product(c, j):
            places = slice(N_TILE * c + P * j, N_TILE * c + P * (j + 1))
            g_acc = psum.tile([P, D], F32, tag="bank")
            for kp in range(A_PASSES):
                nc.tensor.matmul_mx(
                    out=g_acc[:],
                    lhsT=a_codes[:, kp, places].bitcast(FP8X4),
                    lhsT_scale=a_planes[:, kp, places],
                    rhs=w_codes["g"][:, kp, :].bitcast(FP8X4),
                    rhs_scale=w_planes["g"][:, kp, :],
                    start=(kp == 0),
                    stop=(kp == A_PASSES - 1),
                )
            return g_acc

        def g_finish(c, j, g_acc):
            if j == 0:
                g_outs[c] = outs.tile([P, J, D], F32, name="g_out", bufs=G_BUFS)
            g_out = g_outs[c]
            nc.vector.tensor_tensor(out=g_out[:, j, :], in0=g_acc[:], in1=g_bias[:, c, :], op=ADD)

        def store_g(c, js):
            out_rows = out_1[0, N_TILE * c : N_TILE * (c + 1), :].rearrange("(q j) d -> q j d", j=J)
            nc.sync.dma_start(out=out_rows[:, js, :], in_=g_outs[c][:, js, :])

        def g_tile(c, j):
            g_finish(c, j, g_product(c, j))

        def phi_tile(c, m):
            n_cols = slice(N_TILE * c, N_TILE * (c + 1))
            d_rows = slice(P * m, P * (m + 1))
            phi_acc = psum.tile([P, N_TILE], F32, tag="bank")
            for kp in range(A_PASSES):
                nc.tensor.matmul_mx(
                    out=phi_acc[:],
                    lhsT=w_codes["p"][:, kp, d_rows].bitcast(FP8X4),
                    lhsT_scale=w_planes["p"][:, kp, d_rows],
                    rhs=a_codes[:, kp, n_cols].bitcast(FP8X4),
                    rhs_scale=a_planes[:, kp, n_cols],
                    start=(kp == 0),
                    stop=(kp == A_PASSES - 1),
                )
            by_column = phi_acc[:].rearrange("p (j i x) -> p i x j", j=J, i=T_PER_CHUNK)
            phi_out = outs.tile([P, T_PER_CHUNK, COLS_PER_T // J, J], F32)
            for i in range(T_PER_CHUNK):
                t = T_PER_CHUNK * c + i
                nc.scalar.activation(
                    out=phi_out[:, i], in_=by_column[:, i], func=IDENTITY, bias=phi_bias[:, m, t : t + 1]
                )
            nc.sync.dma_start(out=out_0[0, d_rows, n_cols], in_=phi_out[:].rearrange("p i x j -> p (i x j)"))

        passes = range(A_PASSES + Z_PASSES)
        spread_biases()
        for kp in passes:
            quantise_weight("g", 0, kp, flip_weight("g", 0, kp))
        for kp in range(Z_PASSES):
            for s in (2 * kp, 2 * kp + 1):
                finish_fold(s, fold_slab(s))
            scale_video(kp, "vector")
        quantise_video()
        widen_video([0])
        flipped = [flip_weight("g", 1, kp) for kp in passes]
        grouped = [regroup_audio(0, 0, "vector"), regroup_audio(0, 1, "scalar")]
        for kp in passes:
            quantise_weight("g", 1, kp, flipped[kp])
        quantise_audio(0, 0, grouped[0])
        flipped = [flip_weight("p", 0, kp) for kp in passes]
        quantise_audio(0, 1, grouped[1])
        widen_video([1, 2, 3])
        for kp in passes:
            quantise_weight("p", 0, kp, flipped[kp])
        flipped = [flip_weight("p", 1, kp) for kp in passes]
        z_g = video_rows_for_g(0)
        for kp in passes:
            quantise_weight("p", 1, kp, flipped[kp])
        z_phi = [video_columns_for_phi(half) for half in range(2)]
        join_bias_for_g(0, z_g)
        for half in range(2):
            join_bias_for_phi(half, z_phi[half])
        for c in range(CHUNKS):
            if c + 1 < CHUNKS:
                grouped = [regroup_audio(c + 1, 0, ("vector", "vector", "scalar")[c]), None]
                grouped[1] = regroup_audio(c + 1, 1, ("scalar", "scalar", "gpsimd")[c])
                g_tile(c, 0)
                phi_tile(c, 0)
                quantise_audio(c + 1, 0, grouped[0])
                phi_tile(c, 1)
                g_tile(c, 1)
                phi_tile(c, 2)
                quantise_audio(c + 1, 1, grouped[1])
                phi_tile(c, 3)
                g_tile(c, 2)
                g_tile(c, 3)
                store_g(c, slice(0, 2))
                store_g(c, slice(2, 4))
                join_bias_for_g(c + 1, video_rows_for_g(c + 1))
            else:
                phi_tile(c, 0)
                g_tile(c, 0)
                phi_tile(c, 1)
                g_tile(c, 1)
                store_g(c, slice(0, 2))
                phi_tile(c, 2)
                g_tile(c, 2)
                phi_tile(c, 3)
                g_tile(c, 3)
                store_g(c, slice(2, 4))
